import numpy as np
import ml_dtypes


def mxq(x, axis, fmt="e4m3"):
    dtype, down = {"e4m3": (ml_dtypes.float8_e4m3fn, 7), "e5m2": (ml_dtypes.float8_e5m2, 14)}[fmt]
    v = np.moveaxis(np.asarray(x, np.float32).astype(ml_dtypes.bfloat16).astype(np.float64), axis, -1)
    blocks = v.reshape(v.shape[:-1] + (-1, 32))
    amax = np.abs(blocks).max(-1, keepdims=True)
    byte = np.maximum(np.where(amax > 0, np.frexp(amax)[1] - 1 + 127, 0) - down, 1)
    scale = np.exp2(byte - 127.0)
    codes = (blocks / scale).astype(np.float32).astype(dtype).astype(np.float64)
    return np.moveaxis((codes * scale).reshape(v.shape), -1, axis)


WIDE = False


def mx_kscale(k):
    if not WIDE:
        return np.ones(k)
    levels = np.array([10, -10, 5, -5, 0])
    a = np.random.permutation(np.resize(levels, k // 512 * 4)).reshape(k // 512, 4)
    idx = np.arange(k)
    return np.exp2(a[idx // 512, idx % 128 // 32])


BF16 = ml_dtypes.bfloat16


def bf(x):
    return np.asarray(x, np.float32).astype(BF16)


def f64(x):
    return np.asarray(x).astype(np.float64)


B, J, C, K, H = 16, 256, 512, 2, 256
KJ = K * J
EPS = 1e-5


def layernorm(v, g, b):
    m = v.mean(-1, keepdims=True)
    var = v.var(-1, keepdims=True)
    return (v - m) / np.sqrt(var + EPS) * g + b


def gcn(xin, adj, spatial_adj, conv_w, conv_b, s_ctx):
    h = (mxq(xin, 2, "e4m3") @ mxq(conv_w, 1, "e4m3").T) + conv_b
    h = h.reshape(B, J, K, C).transpose(0, 2, 1, 3).reshape(B, KJ, C)
    sadj = np.broadcast_to(spatial_adj[None], (B, K - 1, J, J))
    adj4 = np.concatenate([adj * s_ctx, sadj], axis=1).reshape(B, KJ, J)
    return mxq(adj4, 1, "e4m3").transpose(0, 2, 1) @ mxq(h, 1, "e4m3")


def setup_inputs():
    s = mx_kscale(C)
    t = np.sort(mx_kscale(KJ))[np.arange(K) * (KJ - 1) // (K - 1)]
    tw = np.repeat(t, C)
    a = 2.0 / np.sqrt(KJ)
    return {"g1": bf(np.random.standard_normal((B, J, C)) * 0.9 * s),
            "res1": bf(np.random.standard_normal((B, J, C))),
            "adj": bf(np.random.random((B, 1, J, J)) * a / t[0]),
            "spatial_adj": bf(np.random.random((K - 1, J, J)) * a / t[1:, None, None]),
            "conv2_w": bf(np.random.standard_normal((K * C, C)) / np.sqrt(C) / s[None, :] * tw[:, None]),
            "conv2_b": bf(np.random.standard_normal(K * C) * 0.05 * tw),
            "s2": bf(1.5 + 0.1 * np.random.standard_normal(1)),
            "norm2_g": bf(1.0 + 0.1 * np.random.standard_normal(C)),
            "norm2_b": bf(0.1 * np.random.standard_normal(C))}


def reference(g1, res1, adj, spatial_adj, conv2_w, conv2_b, s2, norm2_g, norm2_b):
    g2 = gcn(f64(g1), f64(adj), f64(spatial_adj), f64(conv2_w), f64(conv2_b), f64(s2))
    x2 = f64(res1) + g2
    xn = layernorm(x2, f64(norm2_g), f64(norm2_b))
    return x2, xn

@@ -1,0 +1,425 @@
+from contextlib import ExitStack
+
+import concourse.mybir as mybir
+from concourse.masks import make_identity
+
+F32 = mybir.dt.float32
+BF16 = mybir.dt.bfloat16
+U32 = mybir.dt.uint32
+U8 = mybir.dt.uint8
+I32 = mybir.dt.int32
+FP8X4 = mybir.dt.float8_e4m3fn_x4
+ALU = mybir.AluOpType
+ACT = mybir.ActivationFunctionType
+
+B = 16
+J = 256
+C = 512
+K = 2
+EPS = 1e-5
+P = 128
+HALF = 64
+PACK = 4
+G1_BUFS = 3
+A_BUFS = 2
+VECTOR_TAIL = 3
+
+FLOPS = 2 * B * J * C * (K * C) + 2 * B * (K * J) * J * C
+
+
+def tile_block_attention_guide_pb_t_kernel(
+    tc, g1, res1, adj, spatial_adj, conv2_w, conv2_b, s2, norm2_g, norm2_b, out_0, out_1
+):
+    nc = tc.nc
+    with ExitStack() as ctx:
+        consts = ctx.enter_context(tc.tile_pool(name="consts", bufs=1))
+        inputs = ctx.enter_context(tc.tile_pool(name="inputs", bufs=1))
+        stage = ctx.enter_context(tc.tile_pool(name="stage", bufs=2))
+        packed = ctx.enter_context(tc.tile_pool(name="packed", bufs=3))
+        results = ctx.enter_context(tc.tile_pool(name="results", bufs=5))
+        stats = ctx.enter_context(tc.tile_pool(name="stats", bufs=4))
+        psum_turn = ctx.enter_context(tc.psum_pool(name="psum_turn", bufs=2))
+        psum_h = ctx.enter_context(tc.psum_pool(name="psum_h", bufs=4))
+        psum_g2 = ctx.enter_context(tc.psum_pool(name="psum_g2", bufs=2))
+        ctx.enter_context(tc.manual_schedule())
+
+        identity = consts.tile([P, P], F32)
+        make_identity(nc, identity[:])
+        eps = consts.tile([P, 1], F32)
+        nc.vector.memset(eps[:], EPS)
+
+        bias_by_parity = consts.tile([P, 2, C], BF16)
+        for parity in range(2):
+            low = parity
+            high = 1 - parity
+            nc.scalar.dma_start(
+                out=bias_by_parity[0:HALF, parity, :],
+                in_=conv2_b[low * C : (low + 1) * C].partition_broadcast(HALF),
+            )
+            nc.scalar.dma_start(
+                out=bias_by_parity[HALF:P, parity, :],
+                in_=conv2_b[high * C : (high + 1) * C].partition_broadcast(HALF),
+            )
+        s2_bf16 = consts.tile([P, 1], BF16)
+        nc.scalar.dma_start(out=s2_bf16[:], in_=s2.partition_broadcast(P))
+        gain = consts.tile([P, C], BF16)
+        nc.scalar.dma_start(out=gain[:], in_=norm2_g.partition_broadcast(P))
+        shift = consts.tile([P, C], BF16)
+        nc.scalar.dma_start(out=shift[:], in_=norm2_b.partition_broadcast(P))
+        first_sqrt = consts.tile([P, 1], F32)
+        nc.scalar.activation(out=first_sqrt[:], in_=eps[:], func=ACT.Sqrt)
+
+        g1_codes = [
+            consts.tile([P, 9 * HALF], U32, name="g1_codes%d" % n, align_bytes=64)
+            for n in range(G1_BUFS)
+        ]
+        g1_scales = [
+            consts.tile([P, 9 * HALF], U8, name="g1_scales%d" % n, align_bytes=64)
+            for n in range(G1_BUFS)
+        ]
+        for n in range(G1_BUFS):
+            nc.vector.memset(g1_codes[n][:].bitcast(I32), 0)
+            nc.vector.memset(g1_scales[n][:].bitcast(I32), 0)
+        s2_f32 = consts.tile([P, 1], F32)
+        nc.vector.tensor_copy(out=s2_f32[:], in_=s2_bf16[:])
+
+        w_raw = consts.tile([P, PACK, K, C], BF16)
+        w_grouped = consts.tile([P, K * C * PACK], BF16, align_bytes=64)
+        w_codes = consts.tile([P, K * C], U32, align_bytes=64)
+        w_scales = consts.tile([P, K * C], U8, align_bytes=64)
+
+        def load_weights():
+            for cc in range(PACK):
+                nc.sync.dma_start(
+                    out=w_raw[:, cc],
+                    in_=conv2_w.rearrange("(k t p) c -> t p k c", k=K, p=P)[cc],
+                )
+
+        def prepare_weights():
+            for cc in range(PACK):
+                turned_w = psum_turn.tile([P, K, 2, P], F32, tag="turned")
+                for k in range(K):
+                    for u in range(2):
+                        nc.tensor.transpose(
+                            turned_w[:, k, u, :],
+                            w_raw[:, cc, k, :].bitcast(F32)[:, u * P : (u + 1) * P],
+                            identity[:],
+                        )
+                cols = slice(cc * K * P * PACK, (cc + 1) * K * P * PACK)
+                nc.scalar.copy(
+                    out=w_grouped[:, cols].bitcast(F32).rearrange("q (k p u) -> q k p u", k=K, u=2),
+                    in_=turned_w[:].rearrange("q k u p -> q k p u"),
+                )
+                nc.vector.quantize_mx(
+                    out=w_codes[:, cc * K * P : (cc + 1) * K * P].bitcast(FP8X4),
+                    scales=w_scales[:, cc * K * P : (cc + 1) * K * P],
+                    in_=w_grouped[:, cols],
+                )
+
+        spatial_raw = consts.tile([P, PACK, J], BF16)
+        a_grouped = [
+            consts.tile([P, 2, J, PACK], BF16, name="a_grouped%d" % n, align_bytes=64)
+            for n in range(A_BUFS)
+        ]
+
+        def load_spatial():
+            for half in range(2):
+                nc.sync.dma_start(
+                    out=spatial_raw[half * HALF : (half + 1) * HALF],
+                    in_=spatial_adj[0].rearrange("(r t) w -> r t w", t=PACK),
+                )
+
+        def place_spatial():
+            for n in range(A_BUFS):
+                for parity in range(2):
+                    rows = slice((1 - parity) * HALF, (2 - parity) * HALF)
+                    nc.gpsimd.tensor_scalar(
+                        out=a_grouped[n][rows, parity],
+                        in0=spatial_raw[rows].rearrange("p t w -> p w t"),
+                        scalar1=1.0,
+                        scalar2=0.0,
+                        op0=ALU.mult,
+                        op1=ALU.add,
+                    )
+
+        g1_raw = {}
+        res_raw = {}
+        adj_raw = {}
+        g1_grouped = {}
+        a_codes = {}
+        a_scales = {}
+        h_acc = {}
+        h_grouped = {}
+        h_codes = {}
+        h_scales = {}
+        g2_acc = {}
+        x2 = {}
+        row_sum = {}
+        neg_mean = {}
+        std = {}
+        rstd = {}
+        neg_mean_rstd = {}
+
+        def load_g1(b):
+            g1_raw[b] = inputs.tile([P, 2, C], BF16, name="g1_raw%d" % b)
+            nc.sync.dma_start(out=g1_raw[b][:], in_=g1[b].rearrange("(t p) c -> p t c", p=P))
+
+        def load_adj(pair):
+            adj_raw[pair] = inputs.tile([P, PACK, J], BF16, name="adj_raw%d" % pair)
+            nc.sync.dma_start(
+                out=adj_raw[pair][:],
+                in_=adj[2 * pair : 2 * pair + 2, 0].rearrange("b (r t) w -> (b r) t w", t=PACK),
+            )
+
+        def load_res(b):
+            res_raw[b] = inputs.tile([P, 2, C], BF16, name="res_raw%d" % b)
+            nc.sync.dma_start(out=res_raw[b][:], in_=res1[b].rearrange("(t p) c -> p t c", p=P))
+
+        def turn_g1(b):
+            turned = psum_turn.tile([P, 2, J], F32, tag="turned")
+            for u in range(2):
+                for jt in range(2):
+                    nc.tensor.transpose(
+                        turned[:, u, jt * P : (jt + 1) * P],
+                        g1_raw[b][:, jt, :].bitcast(F32)[:, u * P : (u + 1) * P],
+                        identity[:],
+                    )
+            grouped = stage.tile([P, J * PACK], BF16, tag="g1_grouped", align_bytes=64)
+            nc.scalar.copy(
+                out=grouped[:].bitcast(F32).rearrange("q (t r u) -> q t r u", t=PACK, u=2),
+                in_=turned[:].rearrange("q u (r t) -> q t r u", t=PACK),
+            )
+            g1_grouped[b] = grouped
+
+        def quantise_g1(b):
+            for t in range(PACK):
+                cols = slice(HALF + t * P, P + t * P)
+                nc.vector.quantize_mx(
+                    out=g1_codes[b % G1_BUFS][:, cols].bitcast(FP8X4),
+                    scales=g1_scales[b % G1_BUFS][:, cols],
+                    in_=g1_grouped[b][:, t * HALF * PACK : (t + 1) * HALF * PACK],
+                )
+
+        def scale_adj(pair):
+            for parity in range(2):
+                rows = slice(parity * HALF, (parity + 1) * HALF)
+                nc.scalar.activation(
+                    out=a_grouped[pair % A_BUFS][rows, parity],
+                    in_=adj_raw[pair][rows].rearrange("p t w -> p w t"),
+                    func=ACT.Copy,
+                    scale=s2_f32[rows, :],
+                )
+
+        def quantise_adj(pair):
+            codes = packed.tile([P, 2 * J], U32, tag="a_codes", align_bytes=64)
+            scales = packed.tile([P, 2 * J], U8, tag="a_scales", align_bytes=64)
+            nc.vector.quantize_mx(
+                out=codes[:].bitcast(FP8X4),
+                scales=scales[:],
+                in_=a_grouped[pair % A_BUFS][:].rearrange("p s w t -> p (s w t)"),
+            )
+            a_codes[pair] = codes
+            a_scales[pair] = scales
+
+        def conv(b, cc):
+            codes = g1_codes[b % G1_BUFS]
+            scales = g1_scales[b % G1_BUFS]
+            k_low = b % 2
+            k_high = 1 - k_low
+            acc = psum_h.tile([P, PACK, P], F32, tag="h_acc")
+            for t in range(PACK):
+                set_then_zero = slice(HALF + t * P, HALF + (t + 1) * P)
+                zero_then_set = slice(t * P, (t + 1) * P)
+                low_cols = slice((K * cc + k_low) * P, (K * cc + k_low + 1) * P)
+                high_cols = slice((K * cc + k_high) * P, (K * cc + k_high + 1) * P)
+                nc.tensor.matmul_mx(
+                    out=acc[:, t, :],
+                    lhsT=codes[:, set_then_zero].bitcast(FP8X4),
+                    lhsT_scale=scales[:, set_then_zero],
+                    rhs=w_codes[:, low_cols].bitcast(FP8X4),
+                    rhs_scale=w_scales[:, low_cols],
+                    start=True,
+                    stop=False,
+                )
+                nc.tensor.matmul_mx(
+                    out=acc[:, t, :],
+                    lhsT=codes[:, zero_then_set].bitcast(FP8X4),
+                    lhsT_scale=scales[:, zero_then_set],
+                    rhs=w_codes[:, high_cols].bitcast(FP8X4),
+                    rhs_scale=w_scales[:, high_cols],
+                    start=False,
+                    stop=True,
+                )
+            h_acc[(b, cc)] = acc
+
+        def add_bias(b, cc):
+            if cc == 0:
+                grouped = stage.tile([P, C, PACK], BF16, tag="h_grouped", align_bytes=64)
+                h_grouped[b] = grouped
+            cols = slice(cc * P, (cc + 1) * P)
+            nc.vector.tensor_tensor(
+                out=h_grouped[b][:, cols, :],
+                in0=h_acc[(b, cc)][:].rearrange("p t c -> p c t"),
+                in1=bias_by_parity[:, b % 2, cols].unsqueeze(2).to_broadcast([P, P, PACK]),
+                op=ALU.add,
+            )
+
+        def quantise_h(b):
+            codes = packed.tile([P, C], U32, tag="h_codes", align_bytes=64)
+            scales = packed.tile([P, C], U8, tag="h_scales", align_bytes=64)
+            nc.vector.quantize_mx(
+                out=codes[:].bitcast(FP8X4),
+                scales=scales[:],
+                in_=h_grouped[b][:].rearrange("p c t -> p (c t)"),
+            )
+            h_codes[b] = codes
+            h_scales[b] = scales
+
+        def aggregate(b):
+            for wt in range(2):
+                cols = slice((b % 2) * J + wt * P, (b % 2) * J + (wt + 1) * P)
+                acc = psum_g2.tile([P, C], F32, tag="g2_acc")
+                nc.tensor.matmul_mx(
+                    out=acc[:],
+                    lhsT=a_codes[b // 2][:, cols].bitcast(FP8X4),
+                    lhsT_scale=a_scales[b // 2][:, cols],
+                    rhs=h_codes[b][:].bitcast(FP8X4),
+                    rhs_scale=h_scales[b][:],
+                    start=True,
+                    stop=True,
+                )
+                g2_acc[(b, wt)] = acc
+
+        def add_residual(b):
+            x2_tile = results.tile([P, 2, C], F32, tag="x2")
+            sums = stats.tile([P, 2], F32, tag="row_sum")
+            for wt in range(2):
+                nc.vector.scalar_tensor_tensor(
+                    out=x2_tile[:, wt, :],
+                    in0=g2_acc[(b, wt)][:],
+                    scalar=1.0,
+                    in1=res_raw[b][:, wt, :],
+                    op0=ALU.mult,
+                    op1=ALU.add,
+                    accum_out=sums[:, wt : wt + 1],
+                )
+            nc.sync.dma_start(out=out_0[b].rearrange("(t p) c -> p t c", p=P), in_=x2_tile[:])
+            x2[b] = x2_tile
+            row_sum[b] = sums
+
+        def deviation(b):
+            minus_mean = stats.tile([P, 2], F32, tag="neg_mean")
+            nc.scalar.activation(out=minus_mean[:], in_=row_sum[b][:], func=ACT.Copy, scale=-1.0 / C)
+            squares = stats.tile([P, 2], F32, tag="squares")
+            for wt in range(2):
+                unread = stats.tile([P, C], BF16, tag="unread")
+                nc.scalar.activation(
+                    out=unread[:],
+                    in_=x2[b][:, wt, :],
+                    func=ACT.Square,
+                    bias=minus_mean[:, wt : wt + 1],
+                    scale=1.0,
+                    accum_out=squares[:, wt : wt + 1],
+                )
+            deviation_tile = stats.tile([P, 2], F32, tag="std")
+            nc.scalar.activation(
+                out=deviation_tile[:], in_=squares[:], func=ACT.Sqrt, bias=eps[:], scale=1.0 / C
+            )
+            neg_mean[b] = minus_mean
+            std[b] = deviation_tile
+
+        def invert_deviation(b):
+            inverse = stats.tile([P, 2], F32, tag="rstd")
+            nc.vector.reciprocal(out=inverse[:], in_=std[b][:])
+            rstd[b] = inverse
+            if b < B - VECTOR_TAIL:
+                offset = stats.tile([P, 2], F32, tag="neg_mean_rstd")
+                nc.vector.tensor_tensor(
+                    out=offset[:], in0=neg_mean[b][:], in1=inverse[:], op=ALU.mult
+                )
+                neg_mean_rstd[b] = offset
+
+        def normalise(b):
+            xn = results.tile([P, 2, C], F32, tag="xn")
+            if b < B - VECTOR_TAIL:
+                for wt in range(2):
+                    nc.scalar.activation(
+                        out=xn[:, wt, :],
+                        in_=x2[b][:, wt, :],
+                        func=ACT.Identity,
+                        bias=neg_mean_rstd[b][:, wt : wt + 1],
+                        scale=rstd[b][:, wt : wt + 1],
+                    )
+                nc.gpsimd.tensor_tensor(
+                    out=xn[:], in0=xn[:], in1=gain[:].unsqueeze(1).to_broadcast([P, 2, C]), op=ALU.mult
+                )
+                nc.gpsimd.tensor_tensor(
+                    out=xn[:], in0=xn[:], in1=shift[:].unsqueeze(1).to_broadcast([P, 2, C]), op=ALU.add
+                )
+            else:
+                for wt in range(2):
+                    nc.vector.scalar_tensor_tensor(
+                        out=xn[:, wt, :],
+                        in0=x2[b][:, wt, :],
+                        scalar=neg_mean[b][:, wt : wt + 1],
+                        in1=gain[:],
+                        op0=ALU.add,
+                        op1=ALU.mult,
+                    )
+                for wt in range(2):
+                    nc.vector.scalar_tensor_tensor(
+                        out=xn[:, wt, :],
+                        in0=xn[:, wt, :],
+                        scalar=rstd[b][:, wt : wt + 1],
+                        in1=shift[:],
+                        op0=ALU.mult,
+                        op1=ALU.add,
+                    )
+            nc.sync.dma_start(out=out_1[b].rearrange("(t p) c -> p t c", p=P), in_=xn[:])
+
+        def in_range(b):
+            return 0 <= b < B
+
+        def step(i):
+            for cc in range(PACK):
+                if in_range(i):
+                    add_bias(i, cc)
+                if in_range(i + 1):
+                    conv(i + 1, cc)
+            if in_range(i - 1):
+                add_residual(i - 1)
+            if in_range(i - 2):
+                invert_deviation(i - 2)
+            if in_range(i):
+                if i % 2 == 0:
+                    quantise_adj(i // 2)
+                quantise_h(i)
+                aggregate(i)
+            if in_range(i + 2):
+                quantise_g1(i + 2)
+            if in_range(i - 1):
+                deviation(i - 1)
+            if in_range(i - 2):
+                normalise(i - 2)
+            if in_range(i + 3):
+                turn_g1(i + 3)
+            if in_range(i + 2) and i % 2 == 0:
+                scale_adj((i + 2) // 2)
+
+        load_g1(0)
+        load_weights()
+        load_adj(0)
+        load_spatial()
+        for b in range(1, B + 4):
+            if in_range(b):
+                load_g1(b)
+                if b % 2 == 0:
+                    load_adj(b // 2)
+            if in_range(b - 4):
+                load_res(b - 4)
+
+        step(-3)
+        prepare_weights()
+        place_spatial()
+        for i in range(-2, B + 2):
+            step(i)

@@ -22,7 +22,7 @@ HALF = 64
 PACK = 4
 G1_BUFS = 3
 A_BUFS = 2
-VECTOR_TAIL = 3
+VECTOR_TAIL = 16
 
 FLOPS = 2 * B * J * C * (K * C) + 2 * B * (K * J) * J * C
 

@@ -22,7 +22,7 @@ HALF = 64
 PACK = 4
 G1_BUFS = 3
 A_BUFS = 2
-VECTOR_TAIL = 16
+VECTOR_TAIL = 3
 
 FLOPS = 2 * B * J * C * (K * C) + 2 * B * (K * J) * J * C
 
@@ -128,6 +128,14 @@ def tile_block_attention_guide_pb_t_kernel(
                     out=spatial_raw[half * HALF : (half + 1) * HALF],
                     in_=spatial_adj[0].rearrange("(r t) w -> r t w", t=PACK),
                 )
+
+        gain_f32 = consts.tile([P, 2, C], F32)
+        shift_f32 = consts.tile([P, 2, C], F32)
+
+        def widen_gain_and_shift():
+            for wt in range(2):
+                nc.vector.tensor_copy(out=gain_f32[:, wt, :], in_=gain[:])
+                nc.vector.tensor_copy(out=shift_f32[:, wt, :], in_=shift[:])
 
         def place_spatial():
             for n in range(A_BUFS):
@@ -340,22 +348,20 @@ def tile_block_attention_guide_pb_t_kernel(
                 neg_mean_rstd[b] = offset
 
         def normalise(b):
-            xn = results.tile([P, 2, C], F32, tag="xn")
+            xn = results.tile([P, 2, C], F32, tag="xn", bufs=3)
             if b < B - VECTOR_TAIL:
+                normal = results.tile([P, 2, C], F32, tag="normal", bufs=3)
+                scaled = results.tile([P, 2, C], F32, tag="scaled", bufs=2)
                 for wt in range(2):
                     nc.scalar.activation(
-                        out=xn[:, wt, :],
+                        out=normal[:, wt, :],
                         in_=x2[b][:, wt, :],
                         func=ACT.Identity,
                         bias=neg_mean_rstd[b][:, wt : wt + 1],
                         scale=rstd[b][:, wt : wt + 1],
                     )
-                nc.gpsimd.tensor_tensor(
-                    out=xn[:], in0=xn[:], in1=gain[:].unsqueeze(1).to_broadcast([P, 2, C]), op=ALU.mult
-                )
-                nc.gpsimd.tensor_tensor(
-                    out=xn[:], in0=xn[:], in1=shift[:].unsqueeze(1).to_broadcast([P, 2, C]), op=ALU.add
-                )
+                nc.gpsimd.tensor_tensor(out=scaled[:], in0=normal[:], in1=gain_f32[:], op=ALU.mult)
+                nc.gpsimd.tensor_tensor(out=xn[:], in0=scaled[:], in1=shift_f32[:], op=ALU.add)
             else:
                 for wt in range(2):
                     nc.vector.scalar_tensor_tensor(
@@ -421,5 +427,6 @@ def tile_block_attention_guide_pb_t_kernel(
         step(-3)
         prepare_weights()
         place_spatial()
+        widen_gain_and_shift()
         for i in range(-2, B + 2):
             step(i)

@@ -22,7 +22,7 @@ HALF = 64
 PACK = 4
 G1_BUFS = 3
 A_BUFS = 2
-VECTOR_TAIL = 3
+VECTOR_EVERY = 4
 
 FLOPS = 2 * B * J * C * (K * C) + 2 * B * (K * J) * J * C
 
@@ -95,9 +95,9 @@ def tile_block_attention_guide_pb_t_kernel(
                     in_=conv2_w.rearrange("(k t p) c -> t p k c", k=K, p=P)[cc],
                 )
 
-        def prepare_weights():
+        def turn_weights():
             for cc in range(PACK):
-                turned_w = psum_turn.tile([P, K, 2, P], F32, tag="turned")
+                turned_w = psum_h.tile([P, K, 2, P], F32, tag="h_acc")
                 for k in range(K):
                     for u in range(2):
                         nc.tensor.transpose(
@@ -106,10 +106,16 @@ def tile_block_attention_guide_pb_t_kernel(
                             identity[:],
                         )
                 cols = slice(cc * K * P * PACK, (cc + 1) * K * P * PACK)
-                nc.scalar.copy(
-                    out=w_grouped[:, cols].bitcast(F32).rearrange("q (k p u) -> q k p u", k=K, u=2),
-                    in_=turned_w[:].rearrange("q k u p -> q k p u"),
-                )
+                pairs_out = w_grouped[:, cols].bitcast(F32).rearrange("q (k p u) -> q k p u", k=K, u=2)
+                pairs_in = turned_w[:].rearrange("q k u p -> q k p u")
+                if cc % 2 == 0:
+                    nc.vector.tensor_copy(out=pairs_out, in_=pairs_in)
+                else:
+                    nc.scalar.copy(out=pairs_out, in_=pairs_in)
+
+        def quantise_weights():
+            for cc in range(PACK):
+                cols = slice(cc * K * P * PACK, (cc + 1) * K * P * PACK)
                 nc.vector.quantize_mx(
                     out=w_codes[:, cc * K * P : (cc + 1) * K * P].bitcast(FP8X4),
                     scales=w_scales[:, cc * K * P : (cc + 1) * K * P],
@@ -128,14 +134,6 @@ def tile_block_attention_guide_pb_t_kernel(
                     out=spatial_raw[half * HALF : (half + 1) * HALF],
                     in_=spatial_adj[0].rearrange("(r t) w -> r t w", t=PACK),
                 )
-
-        gain_f32 = consts.tile([P, 2, C], F32)
-        shift_f32 = consts.tile([P, 2, C], F32)
-
-        def widen_gain_and_shift():
-            for wt in range(2):
-                nc.vector.tensor_copy(out=gain_f32[:, wt, :], in_=gain[:])
-                nc.vector.tensor_copy(out=shift_f32[:, wt, :], in_=shift[:])
 
         def place_spatial():
             for n in range(A_BUFS):
@@ -340,7 +338,7 @@ def tile_block_attention_guide_pb_t_kernel(
             inverse = stats.tile([P, 2], F32, tag="rstd")
             nc.vector.reciprocal(out=inverse[:], in_=std[b][:])
             rstd[b] = inverse
-            if b < B - VECTOR_TAIL:
+            if b % VECTOR_EVERY != VECTOR_EVERY - 1:
                 offset = stats.tile([P, 2], F32, tag="neg_mean_rstd")
                 nc.vector.tensor_tensor(
                     out=offset[:], in0=neg_mean[b][:], in1=inverse[:], op=ALU.mult
@@ -348,20 +346,22 @@ def tile_block_attention_guide_pb_t_kernel(
                 neg_mean_rstd[b] = offset
 
         def normalise(b):
-            xn = results.tile([P, 2, C], F32, tag="xn", bufs=3)
-            if b < B - VECTOR_TAIL:
-                normal = results.tile([P, 2, C], F32, tag="normal", bufs=3)
-                scaled = results.tile([P, 2, C], F32, tag="scaled", bufs=2)
+            xn = results.tile([P, 2, C], F32, tag="xn")
+            if b % VECTOR_EVERY != VECTOR_EVERY - 1:
                 for wt in range(2):
                     nc.scalar.activation(
-                        out=normal[:, wt, :],
+                        out=xn[:, wt, :],
                         in_=x2[b][:, wt, :],
                         func=ACT.Identity,
                         bias=neg_mean_rstd[b][:, wt : wt + 1],
                         scale=rstd[b][:, wt : wt + 1],
                     )
-                nc.gpsimd.tensor_tensor(out=scaled[:], in0=normal[:], in1=gain_f32[:], op=ALU.mult)
-                nc.gpsimd.tensor_tensor(out=xn[:], in0=scaled[:], in1=shift_f32[:], op=ALU.add)
+                nc.gpsimd.tensor_tensor(
+                    out=xn[:], in0=xn[:], in1=gain[:].unsqueeze(1).to_broadcast([P, 2, C]), op=ALU.mult
+                )
+                nc.gpsimd.tensor_tensor(
+                    out=xn[:], in0=xn[:], in1=shift[:].unsqueeze(1).to_broadcast([P, 2, C]), op=ALU.add
+                )
             else:
                 for wt in range(2):
                     nc.vector.scalar_tensor_tensor(
@@ -425,8 +425,9 @@ def tile_block_attention_guide_pb_t_kernel(
                 load_res(b - 4)
 
         step(-3)
-        prepare_weights()
+        turn_weights()
+        step(-2)
+        quantise_weights()
         place_spatial()
-        widen_gain_and_shift()
-        for i in range(-2, B + 2):
+        for i in range(-1, B + 2):
             step(i)

@@ -22,7 +22,8 @@ HALF = 64
 PACK = 4
 G1_BUFS = 3
 A_BUFS = 2
-VECTOR_EVERY = 4
+S2_COLS = 64
+VECTOR_EVERY = 2
 
 FLOPS = 2 * B * J * C * (K * C) + 2 * B * (K * J) * J * C
 
@@ -48,26 +49,54 @@ def tile_block_attention_guide_pb_t_kernel(
         eps = consts.tile([P, 1], F32)
         nc.vector.memset(eps[:], EPS)
 
-        bias_by_parity = consts.tile([P, 2, C], BF16)
-        for parity in range(2):
-            low = parity
-            high = 1 - parity
-            nc.scalar.dma_start(
-                out=bias_by_parity[0:HALF, parity, :],
-                in_=conv2_b[low * C : (low + 1) * C].partition_broadcast(HALF),
-            )
-            nc.scalar.dma_start(
-                out=bias_by_parity[HALF:P, parity, :],
-                in_=conv2_b[high * C : (high + 1) * C].partition_broadcast(HALF),
-            )
-        s2_bf16 = consts.tile([P, 1], BF16)
-        nc.scalar.dma_start(out=s2_bf16[:], in_=s2.partition_broadcast(P))
-        gain = consts.tile([P, C], BF16)
-        nc.scalar.dma_start(out=gain[:], in_=norm2_g.partition_broadcast(P))
-        shift = consts.tile([P, C], BF16)
-        nc.scalar.dma_start(out=shift[:], in_=norm2_b.partition_broadcast(P))
+        vector_rows = consts.tile([P, 4 * C + S2_COLS], BF16)
+        nc.vector.memset(vector_rows[:].bitcast(I32), 0)
+        selector = consts.tile([P, P], BF16)
+        nc.vector.memset(selector[:].bitcast(I32), 0)
+        nc.vector.memset(selector[0:1, 0:HALF], 1.0)
+        nc.vector.memset(selector[32:33, HALF:P], 1.0)
+        nc.vector.memset(selector[64:65, :], 1.0)
+        bias_row = conv2_b.rearrange("(o n) -> o n", o=1)
+        nc.scalar.dma_start(out=vector_rows[0:1, 0 : 2 * C], in_=bias_row)
+        nc.scalar.dma_start(out=vector_rows[32:33, 0:C], in_=bias_row[:, C : 2 * C])
+        nc.scalar.dma_start(out=vector_rows[32:33, C : 2 * C], in_=bias_row[:, 0:C])
+        nc.scalar.dma_start(out=vector_rows[64:65, 4 * C : 4 * C + 1], in_=s2.rearrange("(o n) -> o n", o=1))
+        nc.scalar.dma_start(out=vector_rows[64:65, 2 * C : 3 * C], in_=norm2_g.rearrange("(o n) -> o n", o=1))
+        nc.scalar.dma_start(out=vector_rows[64:65, 3 * C : 4 * C], in_=norm2_b.rearrange("(o n) -> o n", o=1))
         first_sqrt = consts.tile([P, 1], F32)
         nc.scalar.activation(out=first_sqrt[:], in_=eps[:], func=ACT.Sqrt)
+
+        bias_by_parity = consts.tile([P, 2, C], BF16)
+        gain = consts.tile([P, C], BF16)
+        shift = consts.tile([P, C], BF16)
+        s2_f32 = consts.tile([P, 1], F32)
+
+        def spread_rows():
+            for parity in range(2):
+                spread = psum_h.tile([P, C], F32, tag="h_acc")
+                nc.tensor.matmul(
+                    out=spread[:],
+                    lhsT=selector[:],
+                    rhs=vector_rows[:, parity * C : (parity + 1) * C],
+                    start=True,
+                    stop=True,
+                )
+                nc.vector.tensor_copy(out=bias_by_parity[:, parity, :], in_=spread[:])
+            spread_s2 = psum_g2.tile([P, S2_COLS], F32, tag="g2_acc")
+            nc.tensor.matmul(
+                out=spread_s2[:], lhsT=selector[:], rhs=vector_rows[:, 4 * C :], start=True, stop=True
+            )
+            nc.scalar.copy(out=s2_f32[:], in_=spread_s2[:, 0:1])
+            for n, spread_to in ((2, gain), (3, shift)):
+                spread = psum_h.tile([P, C], F32, tag="h_acc")
+                nc.tensor.matmul(
+                    out=spread[:],
+                    lhsT=selector[:],
+                    rhs=vector_rows[:, n * C : (n + 1) * C],
+                    start=True,
+                    stop=True,
+                )
+                nc.scalar.copy(out=spread_to[:], in_=spread[:])
 
         g1_codes = [
             consts.tile([P, 9 * HALF], U32, name="g1_codes%d" % n, align_bytes=64)
@@ -80,8 +109,6 @@ def tile_block_attention_guide_pb_t_kernel(
         for n in range(G1_BUFS):
             nc.vector.memset(g1_codes[n][:].bitcast(I32), 0)
             nc.vector.memset(g1_scales[n][:].bitcast(I32), 0)
-        s2_f32 = consts.tile([P, 1], F32)
-        nc.vector.tensor_copy(out=s2_f32[:], in_=s2_bf16[:])
 
         w_raw = consts.tile([P, PACK, K, C], BF16)
         w_grouped = consts.tile([P, K * C * PACK], BF16, align_bytes=64)
@@ -424,6 +451,7 @@ def tile_block_attention_guide_pb_t_kernel(
             if in_range(b - 4):
                 load_res(b - 4)
 
+        spread_rows()
         step(-3)
         turn_weights()
         step(-2)

@@ -23,7 +23,7 @@ PACK = 4
 G1_BUFS = 3
 A_BUFS = 2
 S2_COLS = 64
-VECTOR_EVERY = 2
+VECTOR_EVERY = 4
 
 FLOPS = 2 * B * J * C * (K * C) + 2 * B * (K * J) * J * C
 
@@ -46,8 +46,6 @@ def tile_block_attention_guide_pb_t_kernel(
 
         identity = consts.tile([P, P], F32)
         make_identity(nc, identity[:])
-        eps = consts.tile([P, 1], F32)
-        nc.vector.memset(eps[:], EPS)
 
         vector_rows = consts.tile([P, 4 * C + S2_COLS], BF16)
         nc.vector.memset(vector_rows[:].bitcast(I32), 0)
@@ -56,6 +54,8 @@ def tile_block_attention_guide_pb_t_kernel(
         nc.vector.memset(selector[0:1, 0:HALF], 1.0)
         nc.vector.memset(selector[32:33, HALF:P], 1.0)
         nc.vector.memset(selector[64:65, :], 1.0)
+        eps = consts.tile([P, 1], F32)
+        nc.vector.memset(eps[:], EPS)
         bias_row = conv2_b.rearrange("(o n) -> o n", o=1)
         nc.scalar.dma_start(out=vector_rows[0:1, 0 : 2 * C], in_=bias_row)
         nc.scalar.dma_start(out=vector_rows[32:33, 0:C], in_=bias_row[:, C : 2 * C])
@@ -71,32 +71,25 @@ def tile_block_attention_guide_pb_t_kernel(
         shift = consts.tile([P, C], BF16)
         s2_f32 = consts.tile([P, 1], F32)
 
-        def spread_rows():
-            for parity in range(2):
-                spread = psum_h.tile([P, C], F32, tag="h_acc")
-                nc.tensor.matmul(
-                    out=spread[:],
-                    lhsT=selector[:],
-                    rhs=vector_rows[:, parity * C : (parity + 1) * C],
-                    start=True,
-                    stop=True,
-                )
-                nc.vector.tensor_copy(out=bias_by_parity[:, parity, :], in_=spread[:])
-            spread_s2 = psum_g2.tile([P, S2_COLS], F32, tag="g2_acc")
+        def spread(first_col, width):
+            spread_out = psum_g2.tile([P, width], F32, tag="g2_acc")
             nc.tensor.matmul(
-                out=spread_s2[:], lhsT=selector[:], rhs=vector_rows[:, 4 * C :], start=True, stop=True
+                out=spread_out[:],
+                lhsT=selector[:],
+                rhs=vector_rows[:, first_col : first_col + width],
+                start=True,
+                stop=True,
             )
-            nc.scalar.copy(out=s2_f32[:], in_=spread_s2[:, 0:1])
-            for n, spread_to in ((2, gain), (3, shift)):
-                spread = psum_h.tile([P, C], F32, tag="h_acc")
-                nc.tensor.matmul(
-                    out=spread[:],
-                    lhsT=selector[:],
-                    rhs=vector_rows[:, n * C : (n + 1) * C],
-                    start=True,
-                    stop=True,
-                )
-                nc.scalar.copy(out=spread_to[:], in_=spread[:])
+            return spread_out
+
+        def spread_bias():
+            for parity in range(2):
+                nc.vector.tensor_copy(out=bias_by_parity[:, parity, :], in_=spread(parity * C, C)[:])
+
+        def spread_s2_gain_shift():
+            nc.scalar.copy(out=s2_f32[:], in_=spread(4 * C, S2_COLS)[:, 0:1])
+            nc.scalar.copy(out=gain[:], in_=spread(2 * C, C)[:])
+            nc.scalar.copy(out=shift[:], in_=spread(3 * C, C)[:])
 
         g1_codes = [
             consts.tile([P, 9 * HALF], U32, name="g1_codes%d" % n, align_bytes=64)
@@ -292,8 +285,8 @@ def tile_block_attention_guide_pb_t_kernel(
             cols = slice(cc * P, (cc + 1) * P)
             nc.vector.tensor_tensor(
                 out=h_grouped[b][:, cols, :],
-                in0=h_acc[(b, cc)][:].rearrange("p t c -> p c t"),
-                in1=bias_by_parity[:, b % 2, cols].unsqueeze(2).to_broadcast([P, P, PACK]),
+                in0=bias_by_parity[:, b % 2, cols].unsqueeze(2).to_broadcast([P, P, PACK]),
+                in1=h_acc[(b, cc)][:].rearrange("p t c -> p c t"),
                 op=ALU.add,
             )
 
@@ -329,9 +322,9 @@ def tile_block_attention_guide_pb_t_kernel(
             for wt in range(2):
                 nc.vector.scalar_tensor_tensor(
                     out=x2_tile[:, wt, :],
-                    in0=g2_acc[(b, wt)][:],
+                    in0=res_raw[b][:, wt, :],
                     scalar=1.0,
-                    in1=res_raw[b][:, wt, :],
+                    in1=g2_acc[(b, wt)][:],
                     op0=ALU.mult,
                     op1=ALU.add,
                     accum_out=sums[:, wt : wt + 1],
@@ -361,11 +354,14 @@ def tile_block_attention_guide_pb_t_kernel(
             neg_mean[b] = minus_mean
             std[b] = deviation_tile
 
+        def on_vector(b):
+            return b % VECTOR_EVERY == VECTOR_EVERY - 1 or b == B - 1
+
         def invert_deviation(b):
             inverse = stats.tile([P, 2], F32, tag="rstd")
             nc.vector.reciprocal(out=inverse[:], in_=std[b][:])
             rstd[b] = inverse
-            if b % VECTOR_EVERY != VECTOR_EVERY - 1:
+            if not on_vector(b):
                 offset = stats.tile([P, 2], F32, tag="neg_mean_rstd")
                 nc.vector.tensor_tensor(
                     out=offset[:], in0=neg_mean[b][:], in1=inverse[:], op=ALU.mult
@@ -374,7 +370,7 @@ def tile_block_attention_guide_pb_t_kernel(
 
         def normalise(b):
             xn = results.tile([P, 2, C], F32, tag="xn")
-            if b % VECTOR_EVERY != VECTOR_EVERY - 1:
+            if not on_vector(b):
                 for wt in range(2):
                     nc.scalar.activation(
                         out=xn[:, wt, :],
@@ -451,9 +447,10 @@ def tile_block_attention_guide_pb_t_kernel(
             if in_range(b - 4):
                 load_res(b - 4)
 
-        spread_rows()
         step(-3)
+        spread_bias()
         turn_weights()
+        spread_s2_gain_shift()
         step(-2)
         quantise_weights()
         place_spatial()

@@ -23,7 +23,7 @@ PACK = 4
 G1_BUFS = 3
 A_BUFS = 2
 S2_COLS = 64
-VECTOR_EVERY = 4
+VECTOR_EVERY = 3
 
 FLOPS = 2 * B * J * C * (K * C) + 2 * B * (K * J) * J * C
 

from contextlib import ExitStack

import concourse.mybir as mybir
from concourse.masks import make_identity

F32 = mybir.dt.float32
BF16 = mybir.dt.bfloat16
U32 = mybir.dt.uint32
U8 = mybir.dt.uint8
I32 = mybir.dt.int32
FP8X4 = mybir.dt.float8_e4m3fn_x4
ALU = mybir.AluOpType
ACT = mybir.ActivationFunctionType

B = 16
J = 256
C = 512
K = 2
EPS = 1e-5
P = 128
HALF = 64
PACK = 4
G1_BUFS = 3
A_BUFS = 2
S2_COLS = 64
VECTOR_EVERY = 3

FLOPS = 2 * B * J * C * (K * C) + 2 * B * (K * J) * J * C


def tile_block_attention_guide_pb_t_kernel(
    tc, g1, res1, adj, spatial_adj, conv2_w, conv2_b, s2, norm2_g, norm2_b, out_0, out_1
):
    nc = tc.nc
    with ExitStack() as ctx:
        consts = ctx.enter_context(tc.tile_pool(name="consts", bufs=1))
        inputs = ctx.enter_context(tc.tile_pool(name="inputs", bufs=1))
        stage = ctx.enter_context(tc.tile_pool(name="stage", bufs=2))
        packed = ctx.enter_context(tc.tile_pool(name="packed", bufs=3))
        results = ctx.enter_context(tc.tile_pool(name="results", bufs=5))
        stats = ctx.enter_context(tc.tile_pool(name="stats", bufs=4))
        psum_turn = ctx.enter_context(tc.psum_pool(name="psum_turn", bufs=2))
        psum_h = ctx.enter_context(tc.psum_pool(name="psum_h", bufs=4))
        psum_g2 = ctx.enter_context(tc.psum_pool(name="psum_g2", bufs=2))
        ctx.enter_context(tc.manual_schedule())

        identity = consts.tile([P, P], F32)
        make_identity(nc, identity[:])

        vector_rows = consts.tile([P, 4 * C + S2_COLS], BF16)
        nc.vector.memset(vector_rows[:].bitcast(I32), 0)
        selector = consts.tile([P, P], BF16)
        nc.vector.memset(selector[:].bitcast(I32), 0)
        nc.vector.memset(selector[0:1, 0:HALF], 1.0)
        nc.vector.memset(selector[32:33, HALF:P], 1.0)
        nc.vector.memset(selector[64:65, :], 1.0)
        eps = consts.tile([P, 1], F32)
        nc.vector.memset(eps[:], EPS)
        bias_row = conv2_b.rearrange("(o n) -> o n", o=1)
        nc.scalar.dma_start(out=vector_rows[0:1, 0 : 2 * C], in_=bias_row)
        nc.scalar.dma_start(out=vector_rows[32:33, 0:C], in_=bias_row[:, C : 2 * C])
        nc.scalar.dma_start(out=vector_rows[32:33, C : 2 * C], in_=bias_row[:, 0:C])
        nc.scalar.dma_start(out=vector_rows[64:65, 4 * C : 4 * C + 1], in_=s2.rearrange("(o n) -> o n", o=1))
        nc.scalar.dma_start(out=vector_rows[64:65, 2 * C : 3 * C], in_=norm2_g.rearrange("(o n) -> o n", o=1))
        nc.scalar.dma_start(out=vector_rows[64:65, 3 * C : 4 * C], in_=norm2_b.rearrange("(o n) -> o n", o=1))
        first_sqrt = consts.tile([P, 1], F32)
        nc.scalar.activation(out=first_sqrt[:], in_=eps[:], func=ACT.Sqrt)

        bias_by_parity = consts.tile([P, 2, C], BF16)
        gain = consts.tile([P, C], BF16)
        shift = consts.tile([P, C], BF16)
        s2_f32 = consts.tile([P, 1], F32)

        def spread(first_col, width):
            spread_out = psum_g2.tile([P, width], F32, tag="g2_acc")
            nc.tensor.matmul(
                out=spread_out[:],
                lhsT=selector[:],
                rhs=vector_rows[:, first_col : first_col + width],
                start=True,
                stop=True,
            )
            return spread_out

        def spread_bias():
            for parity in range(2):
                nc.vector.tensor_copy(out=bias_by_parity[:, parity, :], in_=spread(parity * C, C)[:])

        def spread_s2_gain_shift():
            nc.scalar.copy(out=s2_f32[:], in_=spread(4 * C, S2_COLS)[:, 0:1])
            nc.scalar.copy(out=gain[:], in_=spread(2 * C, C)[:])
            nc.scalar.copy(out=shift[:], in_=spread(3 * C, C)[:])

        g1_codes = [
            consts.tile([P, 9 * HALF], U32, name="g1_codes%d" % n, align_bytes=64)
            for n in range(G1_BUFS)
        ]
        g1_scales = [
            consts.tile([P, 9 * HALF], U8, name="g1_scales%d" % n, align_bytes=64)
            for n in range(G1_BUFS)
        ]
        for n in range(G1_BUFS):
            nc.vector.memset(g1_codes[n][:].bitcast(I32), 0)
            nc.vector.memset(g1_scales[n][:].bitcast(I32), 0)

        w_raw = consts.tile([P, PACK, K, C], BF16)
        w_grouped = consts.tile([P, K * C * PACK], BF16, align_bytes=64)
        w_codes = consts.tile([P, K * C], U32, align_bytes=64)
        w_scales = consts.tile([P, K * C], U8, align_bytes=64)

        def load_weights():
            for cc in range(PACK):
                nc.sync.dma_start(
                    out=w_raw[:, cc],
                    in_=conv2_w.rearrange("(k t p) c -> t p k c", k=K, p=P)[cc],
                )

        def turn_weights():
            for cc in range(PACK):
                turned_w = psum_h.tile([P, K, 2, P], F32, tag="h_acc")
                for k in range(K):
                    for u in range(2):
                        nc.tensor.transpose(
                            turned_w[:, k, u, :],
                            w_raw[:, cc, k, :].bitcast(F32)[:, u * P : (u + 1) * P],
                            identity[:],
                        )
                cols = slice(cc * K * P * PACK, (cc + 1) * K * P * PACK)
                pairs_out = w_grouped[:, cols].bitcast(F32).rearrange("q (k p u) -> q k p u", k=K, u=2)
                pairs_in = turned_w[:].rearrange("q k u p -> q k p u")
                if cc % 2 == 0:
                    nc.vector.tensor_copy(out=pairs_out, in_=pairs_in)
                else:
                    nc.scalar.copy(out=pairs_out, in_=pairs_in)

        def quantise_weights():
            for cc in range(PACK):
                cols = slice(cc * K * P * PACK, (cc + 1) * K * P * PACK)
                nc.vector.quantize_mx(
                    out=w_codes[:, cc * K * P : (cc + 1) * K * P].bitcast(FP8X4),
                    scales=w_scales[:, cc * K * P : (cc + 1) * K * P],
                    in_=w_grouped[:, cols],
                )

        spatial_raw = consts.tile([P, PACK, J], BF16)
        a_grouped = [
            consts.tile([P, 2, J, PACK], BF16, name="a_grouped%d" % n, align_bytes=64)
            for n in range(A_BUFS)
        ]

        def load_spatial():
            for half in range(2):
                nc.sync.dma_start(
                    out=spatial_raw[half * HALF : (half + 1) * HALF],
                    in_=spatial_adj[0].rearrange("(r t) w -> r t w", t=PACK),
                )

        def place_spatial():
            for n in range(A_BUFS):
                for parity in range(2):
                    rows = slice((1 - parity) * HALF, (2 - parity) * HALF)
                    nc.gpsimd.tensor_scalar(
                        out=a_grouped[n][rows, parity],
                        in0=spatial_raw[rows].rearrange("p t w -> p w t"),
                        scalar1=1.0,
                        scalar2=0.0,
                        op0=ALU.mult,
                        op1=ALU.add,
                    )

        g1_raw = {}
        res_raw = {}
        adj_raw = {}
        g1_grouped = {}
        a_codes = {}
        a_scales = {}
        h_acc = {}
        h_grouped = {}
        h_codes = {}
        h_scales = {}
        g2_acc = {}
        x2 = {}
        row_sum = {}
        neg_mean = {}
        std = {}
        rstd = {}
        neg_mean_rstd = {}

        def load_g1(b):
            g1_raw[b] = inputs.tile([P, 2, C], BF16, name="g1_raw%d" % b)
            nc.sync.dma_start(out=g1_raw[b][:], in_=g1[b].rearrange("(t p) c -> p t c", p=P))

        def load_adj(pair):
            adj_raw[pair] = inputs.tile([P, PACK, J], BF16, name="adj_raw%d" % pair)
            nc.sync.dma_start(
                out=adj_raw[pair][:],
                in_=adj[2 * pair : 2 * pair + 2, 0].rearrange("b (r t) w -> (b r) t w", t=PACK),
            )

        def load_res(b):
            res_raw[b] = inputs.tile([P, 2, C], BF16, name="res_raw%d" % b)
            nc.sync.dma_start(out=res_raw[b][:], in_=res1[b].rearrange("(t p) c -> p t c", p=P))

        def turn_g1(b):
            turned = psum_turn.tile([P, 2, J], F32, tag="turned")
            for u in range(2):
                for jt in range(2):
                    nc.tensor.transpose(
                        turned[:, u, jt * P : (jt + 1) * P],
                        g1_raw[b][:, jt, :].bitcast(F32)[:, u * P : (u + 1) * P],
                        identity[:],
                    )
            grouped = stage.tile([P, J * PACK], BF16, tag="g1_grouped", align_bytes=64)
            nc.scalar.copy(
                out=grouped[:].bitcast(F32).rearrange("q (t r u) -> q t r u", t=PACK, u=2),
                in_=turned[:].rearrange("q u (r t) -> q t r u", t=PACK),
            )
            g1_grouped[b] = grouped

        def quantise_g1(b):
            for t in range(PACK):
                cols = slice(HALF + t * P, P + t * P)
                nc.vector.quantize_mx(
                    out=g1_codes[b % G1_BUFS][:, cols].bitcast(FP8X4),
                    scales=g1_scales[b % G1_BUFS][:, cols],
                    in_=g1_grouped[b][:, t * HALF * PACK : (t + 1) * HALF * PACK],
                )

        def scale_adj(pair):
            for parity in range(2):
                rows = slice(parity * HALF, (parity + 1) * HALF)
                nc.scalar.activation(
                    out=a_grouped[pair % A_BUFS][rows, parity],
                    in_=adj_raw[pair][rows].rearrange("p t w -> p w t"),
                    func=ACT.Copy,
                    scale=s2_f32[rows, :],
                )

        def quantise_adj(pair):
            codes = packed.tile([P, 2 * J], U32, tag="a_codes", align_bytes=64)
            scales = packed.tile([P, 2 * J], U8, tag="a_scales", align_bytes=64)
            nc.vector.quantize_mx(
                out=codes[:].bitcast(FP8X4),
                scales=scales[:],
                in_=a_grouped[pair % A_BUFS][:].rearrange("p s w t -> p (s w t)"),
            )
            a_codes[pair] = codes
            a_scales[pair] = scales

        def conv(b, cc):
            codes = g1_codes[b % G1_BUFS]
            scales = g1_scales[b % G1_BUFS]
            k_low = b % 2
            k_high = 1 - k_low
            acc = psum_h.tile([P, PACK, P], F32, tag="h_acc")
            for t in range(PACK):
                set_then_zero = slice(HALF + t * P, HALF + (t + 1) * P)
                zero_then_set = slice(t * P, (t + 1) * P)
                low_cols = slice((K * cc + k_low) * P, (K * cc + k_low + 1) * P)
                high_cols = slice((K * cc + k_high) * P, (K * cc + k_high + 1) * P)
                nc.tensor.matmul_mx(
                    out=acc[:, t, :],
                    lhsT=codes[:, set_then_zero].bitcast(FP8X4),
                    lhsT_scale=scales[:, set_then_zero],
                    rhs=w_codes[:, low_cols].bitcast(FP8X4),
                    rhs_scale=w_scales[:, low_cols],
                    start=True,
                    stop=False,
                )
                nc.tensor.matmul_mx(
                    out=acc[:, t, :],
                    lhsT=codes[:, zero_then_set].bitcast(FP8X4),
                    lhsT_scale=scales[:, zero_then_set],
                    rhs=w_codes[:, high_cols].bitcast(FP8X4),
                    rhs_scale=w_scales[:, high_cols],
                    start=False,
                    stop=True,
                )
            h_acc[(b, cc)] = acc

        def add_bias(b, cc):
            if cc == 0:
                grouped = stage.tile([P, C, PACK], BF16, tag="h_grouped", align_bytes=64)
                h_grouped[b] = grouped
            cols = slice(cc * P, (cc + 1) * P)
            nc.vector.tensor_tensor(
                out=h_grouped[b][:, cols, :],
                in0=bias_by_parity[:, b % 2, cols].unsqueeze(2).to_broadcast([P, P, PACK]),
                in1=h_acc[(b, cc)][:].rearrange("p t c -> p c t"),
                op=ALU.add,
            )

        def quantise_h(b):
            codes = packed.tile([P, C], U32, tag="h_codes", align_bytes=64)
            scales = packed.tile([P, C], U8, tag="h_scales", align_bytes=64)
            nc.vector.quantize_mx(
                out=codes[:].bitcast(FP8X4),
                scales=scales[:],
                in_=h_grouped[b][:].rearrange("p c t -> p (c t)"),
            )
            h_codes[b] = codes
            h_scales[b] = scales

        def aggregate(b):
            for wt in range(2):
                cols = slice((b % 2) * J + wt * P, (b % 2) * J + (wt + 1) * P)
                acc = psum_g2.tile([P, C], F32, tag="g2_acc")
                nc.tensor.matmul_mx(
                    out=acc[:],
                    lhsT=a_codes[b // 2][:, cols].bitcast(FP8X4),
                    lhsT_scale=a_scales[b // 2][:, cols],
                    rhs=h_codes[b][:].bitcast(FP8X4),
                    rhs_scale=h_scales[b][:],
                    start=True,
                    stop=True,
                )
                g2_acc[(b, wt)] = acc

        def add_residual(b):
            x2_tile = results.tile([P, 2, C], F32, tag="x2")
            sums = stats.tile([P, 2], F32, tag="row_sum")
            for wt in range(2):
                nc.vector.scalar_tensor_tensor(
                    out=x2_tile[:, wt, :],
                    in0=res_raw[b][:, wt, :],
                    scalar=1.0,
                    in1=g2_acc[(b, wt)][:],
                    op0=ALU.mult,
                    op1=ALU.add,
                    accum_out=sums[:, wt : wt + 1],
                )
            nc.sync.dma_start(out=out_0[b].rearrange("(t p) c -> p t c", p=P), in_=x2_tile[:])
            x2[b] = x2_tile
            row_sum[b] = sums

        def deviation(b):
            minus_mean = stats.tile([P, 2], F32, tag="neg_mean")
            nc.scalar.activation(out=minus_mean[:], in_=row_sum[b][:], func=ACT.Copy, scale=-1.0 / C)
            squares = stats.tile([P, 2], F32, tag="squares")
            for wt in range(2):
                unread = stats.tile([P, C], BF16, tag="unread")
                nc.scalar.activation(
                    out=unread[:],
                    in_=x2[b][:, wt, :],
                    func=ACT.Square,
                    bias=minus_mean[:, wt : wt + 1],
                    scale=1.0,
                    accum_out=squares[:, wt : wt + 1],
                )
            deviation_tile = stats.tile([P, 2], F32, tag="std")
            nc.scalar.activation(
                out=deviation_tile[:], in_=squares[:], func=ACT.Sqrt, bias=eps[:], scale=1.0 / C
            )
            neg_mean[b] = minus_mean
            std[b] = deviation_tile

        def on_vector(b):
            return b % VECTOR_EVERY == VECTOR_EVERY - 1 or b == B - 1

        def invert_deviation(b):
            inverse = stats.tile([P, 2], F32, tag="rstd")
            nc.vector.reciprocal(out=inverse[:], in_=std[b][:])
            rstd[b] = inverse
            if not on_vector(b):
                offset = stats.tile([P, 2], F32, tag="neg_mean_rstd")
                nc.vector.tensor_tensor(
                    out=offset[:], in0=neg_mean[b][:], in1=inverse[:], op=ALU.mult
                )
                neg_mean_rstd[b] = offset

        def normalise(b):
            xn = results.tile([P, 2, C], F32, tag="xn")
            if not on_vector(b):
                for wt in range(2):
                    nc.scalar.activation(
                        out=xn[:, wt, :],
                        in_=x2[b][:, wt, :],
                        func=ACT.Identity,
                        bias=neg_mean_rstd[b][:, wt : wt + 1],
                        scale=rstd[b][:, wt : wt + 1],
                    )
                nc.gpsimd.tensor_tensor(
                    out=xn[:], in0=xn[:], in1=gain[:].unsqueeze(1).to_broadcast([P, 2, C]), op=ALU.mult
                )
                nc.gpsimd.tensor_tensor(
                    out=xn[:], in0=xn[:], in1=shift[:].unsqueeze(1).to_broadcast([P, 2, C]), op=ALU.add
                )
            else:
                for wt in range(2):
                    nc.vector.scalar_tensor_tensor(
                        out=xn[:, wt, :],
                        in0=x2[b][:, wt, :],
                        scalar=neg_mean[b][:, wt : wt + 1],
                        in1=gain[:],
                        op0=ALU.add,
                        op1=ALU.mult,
                    )
                for wt in range(2):
                    nc.vector.scalar_tensor_tensor(
                        out=xn[:, wt, :],
                        in0=xn[:, wt, :],
                        scalar=rstd[b][:, wt : wt + 1],
                        in1=shift[:],
                        op0=ALU.mult,
                        op1=ALU.add,
                    )
            nc.sync.dma_start(out=out_1[b].rearrange("(t p) c -> p t c", p=P), in_=xn[:])

        def in_range(b):
            return 0 <= b < B

        def step(i):
            for cc in range(PACK):
                if in_range(i):
                    add_bias(i, cc)
                if in_range(i + 1):
                    conv(i + 1, cc)
            if in_range(i - 1):
                add_residual(i - 1)
            if in_range(i - 2):
                invert_deviation(i - 2)
            if in_range(i):
                if i % 2 == 0:
                    quantise_adj(i // 2)
                quantise_h(i)
                aggregate(i)
            if in_range(i + 2):
                quantise_g1(i + 2)
            if in_range(i - 1):
                deviation(i - 1)
            if in_range(i - 2):
                normalise(i - 2)
            if in_range(i + 3):
                turn_g1(i + 3)
            if in_range(i + 2) and i % 2 == 0:
                scale_adj((i + 2) // 2)

        load_g1(0)
        load_weights()
        load_adj(0)
        load_spatial()
        for b in range(1, B + 4):
            if in_range(b):
                load_g1(b)
                if b % 2 == 0:
                    load_adj(b // 2)
            if in_range(b - 4):
                load_res(b - 4)

        step(-3)
        spread_bias()
        turn_weights()
        spread_s2_gain_shift()
        step(-2)
        quantise_weights()
        place_spatial()
        for i in range(-1, B + 2):
            step(i)
